import numpy as np
import ml_dtypes

BF16 = ml_dtypes.bfloat16


def bf(x):
    return np.asarray(x, np.float32).astype(BF16)


def f32(x):
    return np.asarray(x, np.float32)


def f64(x):
    return np.asarray(x).astype(np.float64)


def striped(idx):
    return np.tile(idx.reshape(-1, 16).T, (8, 1))


H, D, C, S, T, N = 4, 128, 512, 2048, 2048, 1024


def setup_inputs():
    return {
        "base": f32(0.5 * np.random.standard_normal((C, S))),
        "q": bf(2.0 * np.random.standard_normal((C, N))),
        "k": bf(np.random.standard_normal((C, T))),
        "v": bf(3.0 * np.random.standard_normal((T, C))),
        "offs": striped(np.random.permutation(S)[:N]),
    }


def reference(base, q, k, v, offs):
    idx = offs[:16].T.reshape(-1)
    out = f64(base).copy()
    for h in range(H):
        rows = slice(h * D, (h + 1) * D)
        e = np.exp((f64(k)[rows].T @ f64(q)[rows]) / np.sqrt(D))
        num = f64(v)[:, rows].T @ e
        r = 1.0 / e.sum(axis=0, keepdims=True)
        out[rows, idx] = num * r
    return out

@@ -1,0 +1,69 @@
+import math
+
+import concourse.mybir as mybir
+
+H, D, S, T, N = 4, 128, 2048, 2048, 1024
+P = 128
+JW = 512
+KEY_BLOCKS = T // P
+PIECES = N // JW
+
+FLOPS = 4 * H * D * T * N
+
+BF16, F32, U16 = mybir.dt.bfloat16, mybir.dt.float32, mybir.dt.uint16
+EXP = mybir.ActivationFunctionType.Exp
+MULT = mybir.AluOpType.mult
+
+
+def tile_longcontextattention_b_kernel(tc, base, q, k, v, offs, out):
+    nc = tc.nc
+    v_blocks = v.rearrange("(b p) c -> p b c", p=P)
+    with (
+        tc.tile_pool(name="held", bufs=1) as held,
+        tc.tile_pool(name="weights", bufs=4) as weights,
+        tc.tile_pool(name="results", bufs=2) as results,
+        tc.psum_pool(name="scores", bufs=4) as scores,
+        tc.psum_pool(name="sums", bufs=2) as sums,
+    ):
+        offsets = held.tile([P, N // 16], U16, name="offsets")
+        nc.sync.dma_start(offsets[:], offs)
+
+        q_sb, k_sb, v_sb, window = [], [], [], []
+        for h in range(H):
+            rows = slice(h * D, (h + 1) * D)
+            q_sb.append(held.tile([P, N], BF16, name="q%d" % h))
+            k_sb.append(held.tile([P, T], BF16, name="k%d" % h))
+            v_sb.append(held.tile([P, KEY_BLOCKS, D], BF16, name="v%d" % h))
+            window.append(held.tile([P, S], F32, name="window%d" % h))
+            nc.sync.dma_start(q_sb[h][:], q[rows, :])
+            nc.sync.dma_start(k_sb[h][:], k[rows, :])
+            nc.sync.dma_start(v_sb[h][:], v_blocks[:, :, rows])
+            nc.sync.dma_start(window[h][:], base[rows, :])
+
+        ones = held.tile([P, P], BF16, name="ones")
+        nc.vector.memset(ones[:], 1.0)
+
+        for h in range(H):
+            for piece in range(PIECES):
+                cols = slice(piece * JW, (piece + 1) * JW)
+                num_ps = sums.tile([P, JW], F32, name="num_ps")
+                den_ps = sums.tile([P, JW], F32, name="den_ps")
+                for b in range(KEY_BLOCKS):
+                    first, last = b == 0, b == KEY_BLOCKS - 1
+                    s_ps = scores.tile([P, JW], F32, name="s_ps")
+                    nc.tensor.matmul(s_ps[:], k_sb[h][:, b * P : (b + 1) * P], q_sb[h][:, cols], start=True, stop=True)
+                    e = weights.tile([P, JW], BF16, name="e")
+                    nc.scalar.activation(e[:], s_ps[:], EXP, scale=1.0 / math.sqrt(D))
+                    nc.tensor.matmul(num_ps[:], v_sb[h][:, b, :], e[:], start=first, stop=last)
+                    nc.tensor.matmul(den_ps[:], ones[:], e[:], start=first, stop=last)
+                num = results.tile([P, JW], F32, name="num")
+                nc.vector.tensor_copy(num[:], num_ps[:])
+                r = results.tile([P, JW], F32, name="r")
+                nc.vector.reciprocal(r[:], den_ps[:])
+                nc.vector.tensor_tensor(
+                    window[h][:].indirect(offsets[:, piece * (JW // 16) : (piece + 1) * (JW // 16)]),
+                    num[:],
+                    r[:],
+                    MULT,
+                )
+            nc.sync.dma_start(out[h * D : (h + 1) * D, :], window[h][:])

@@ -1,12 +1,16 @@
 import math
 
 import concourse.mybir as mybir
+from concourse.masks import make_identity
 
 H, D, S, T, N = 4, 128, 2048, 2048, 1024
 P = 128
 JW = 512
 KEY_BLOCKS = T // P
 PIECES = N // JW
+GROUPS = JW // P
+VW = 144
+FW = 256
 
 FLOPS = 4 * H * D * T * N
 
@@ -20,10 +24,12 @@ def tile_longcontextattention_b_kernel(tc, base, q, k, v, offs, out):
     v_blocks = v.rearrange("(b p) c -> p b c", p=P)
     with (
         tc.tile_pool(name="held", bufs=1) as held,
-        tc.tile_pool(name="weights", bufs=4) as weights,
+        tc.tile_pool(name="weights", bufs=6) as weights,
+        tc.tile_pool(name="queries_first", bufs=4) as queries_first,
         tc.tile_pool(name="results", bufs=2) as results,
-        tc.psum_pool(name="scores", bufs=4) as scores,
-        tc.psum_pool(name="sums", bufs=2) as sums,
+        tc.psum_pool(name="scores", bufs=3) as scores,
+        tc.psum_pool(name="products", bufs=1) as products,
+        tc.psum_pool(name="flips", bufs=1) as flips,
     ):
         offsets = held.tile([P, N // 16], U16, name="offsets")
         nc.sync.dma_start(offsets[:], offs)
@@ -33,37 +39,61 @@ def tile_longcontextattention_b_kernel(tc, base, q, k, v, offs, out):
             rows = slice(h * D, (h + 1) * D)
             q_sb.append(held.tile([P, N], BF16, name="q%d" % h))
             k_sb.append(held.tile([P, T], BF16, name="k%d" % h))
-            v_sb.append(held.tile([P, KEY_BLOCKS, D], BF16, name="v%d" % h))
+            v_sb.append(held.tile([P, KEY_BLOCKS, VW], BF16, name="v%d" % h))
             window.append(held.tile([P, S], F32, name="window%d" % h))
+            nc.gpsimd.memset(v_sb[h][:, :, D:VW], 1.0)
             nc.sync.dma_start(q_sb[h][:], q[rows, :])
             nc.sync.dma_start(k_sb[h][:], k[rows, :])
-            nc.sync.dma_start(v_sb[h][:], v_blocks[:, :, rows])
+            nc.sync.dma_start(v_sb[h][:, :, 0:D], v_blocks[:, :, rows])
             nc.sync.dma_start(window[h][:], base[rows, :])
 
-        ones = held.tile([P, P], BF16, name="ones")
-        nc.vector.memset(ones[:], 1.0)
+        identity = held.tile([P, P], F32, name="identity")
+        make_identity(nc, identity[:])
 
         for h in range(H):
             for piece in range(PIECES):
-                cols = slice(piece * JW, (piece + 1) * JW)
-                num_ps = sums.tile([P, JW], F32, name="num_ps")
-                den_ps = sums.tile([P, JW], F32, name="den_ps")
+                product = [products.tile([P, D + 1], F32, name="product%d" % g) for g in range(GROUPS)]
                 for b in range(KEY_BLOCKS):
-                    first, last = b == 0, b == KEY_BLOCKS - 1
                     s_ps = scores.tile([P, JW], F32, name="s_ps")
-                    nc.tensor.matmul(s_ps[:], k_sb[h][:, b * P : (b + 1) * P], q_sb[h][:, cols], start=True, stop=True)
+                    nc.tensor.matmul(
+                        s_ps[:],
+                        k_sb[h][:, b * P : (b + 1) * P],
+                        q_sb[h][:, piece * JW : (piece + 1) * JW],
+                        start=True,
+                        stop=True,
+                    )
                     e = weights.tile([P, JW], BF16, name="e")
                     nc.scalar.activation(e[:], s_ps[:], EXP, scale=1.0 / math.sqrt(D))
-                    nc.tensor.matmul(num_ps[:], v_sb[h][:, b, :], e[:], start=first, stop=last)
-                    nc.tensor.matmul(den_ps[:], ones[:], e[:], start=first, stop=last)
-                num = results.tile([P, JW], F32, name="num")
-                nc.vector.tensor_copy(num[:], num_ps[:])
-                r = results.tile([P, JW], F32, name="r")
-                nc.vector.reciprocal(r[:], den_ps[:])
-                nc.vector.tensor_tensor(
-                    window[h][:].indirect(offsets[:, piece * (JW // 16) : (piece + 1) * (JW // 16)]),
-                    num[:],
-                    r[:],
-                    MULT,
-                )
+                    for g in range(GROUPS):
+                        nc.tensor.matmul(
+                            product[g][:],
+                            e[:, g * P : (g + 1) * P],
+                            v_sb[h][:, b, 0 : D + 1],
+                            start=(b == 0),
+                            stop=(b == KEY_BLOCKS - 1),
+                        )
+
+                num_t = [queries_first.tile([P, D + 1], F32, name="num_t") for g in range(GROUPS)]
+                for g in range(GROUPS):
+                    nc.vector.tensor_copy(num_t[g][:], product[g][:])
+
+                for part in range(JW // FW):
+                    flipped = flips.tile([P, 2, FW], F32, name="flipped")
+                    for i in range(FW // P):
+                        g = part * (FW // P) + i
+                        r_t = queries_first.tile([P, 1], F32, name="r_t")
+                        nc.vector.reciprocal(r_t[:], num_t[g][:, D : D + 1])
+                        r_wide = queries_first.tile([P, P], F32, name="r_wide")
+                        nc.vector.tensor_copy(r_wide[:], r_t[:].to_broadcast([P, P]))
+                        nc.tensor.transpose(flipped[:, 0, i * P : (i + 1) * P], num_t[g][:, 0:D], identity[:])
+                        nc.tensor.transpose(flipped[:, 1, i * P : (i + 1) * P], r_wide[:], identity[:])
+                    num_r = results.tile([P, 2, FW], F32, name="num_r")
+                    nc.vector.tensor_copy(num_r[:], flipped[:])
+                    first = (piece * JW + part * FW) // 16
+                    nc.vector.tensor_tensor(
+                        window[h][:].indirect(offsets[:, first : first + FW // 16]),
+                        num_r[:, 0, :],
+                        num_r[:, 1, :],
+                        MULT,
+                    )
             nc.sync.dma_start(out[h * D : (h + 1) * D, :], window[h][:])

@@ -5,10 +5,8 @@ from concourse.masks import make_identity
 
 H, D, S, T, N = 4, 128, 2048, 2048, 1024
 P = 128
-JW = 512
 KEY_BLOCKS = T // P
-PIECES = N // JW
-GROUPS = JW // P
+BANK_BLOCKS = 4
 VW = 144
 FW = 256
 
@@ -27,12 +25,11 @@ def tile_longcontextattention_b_kernel(tc, base, q, k, v, offs, out):
         tc.tile_pool(name="weights", bufs=6) as weights,
         tc.tile_pool(name="queries_first", bufs=4) as queries_first,
         tc.tile_pool(name="results", bufs=2) as results,
-        tc.psum_pool(name="scores", bufs=3) as scores,
-        tc.psum_pool(name="products", bufs=1) as products,
+        tc.psum_pool(name="scores", bufs=4) as scores,
+        tc.psum_pool(name="products", bufs=3) as products,
         tc.psum_pool(name="flips", bufs=1) as flips,
     ):
         offsets = held.tile([P, N // 16], U16, name="offsets")
-        nc.sync.dma_start(offsets[:], offs)
 
         q_sb, k_sb, v_sb, window = [], [], [], []
         for h in range(H):
@@ -43,57 +40,57 @@ def tile_longcontextattention_b_kernel(tc, base, q, k, v, offs, out):
             window.append(held.tile([P, S], F32, name="window%d" % h))
             nc.gpsimd.memset(v_sb[h][:, :, D:VW], 1.0)
             nc.sync.dma_start(q_sb[h][:], q[rows, :])
-            nc.sync.dma_start(k_sb[h][:], k[rows, :])
+            for c0 in range(0, T, BANK_BLOCKS * P):
+                nc.sync.dma_start(k_sb[h][:, c0 : c0 + BANK_BLOCKS * P], k[rows, c0 : c0 + BANK_BLOCKS * P])
             nc.sync.dma_start(v_sb[h][:, :, 0:D], v_blocks[:, :, rows])
+            if h == 0:
+                nc.sync.dma_start(offsets[:], offs)
             nc.sync.dma_start(window[h][:], base[rows, :])
 
         identity = held.tile([P, P], F32, name="identity")
         make_identity(nc, identity[:])
 
         for h in range(H):
-            for piece in range(PIECES):
-                product = [products.tile([P, D + 1], F32, name="product%d" % g) for g in range(GROUPS)]
-                for b in range(KEY_BLOCKS):
-                    s_ps = scores.tile([P, JW], F32, name="s_ps")
-                    nc.tensor.matmul(
-                        s_ps[:],
-                        k_sb[h][:, b * P : (b + 1) * P],
-                        q_sb[h][:, piece * JW : (piece + 1) * JW],
-                        start=True,
-                        stop=True,
-                    )
-                    e = weights.tile([P, JW], BF16, name="e")
-                    nc.scalar.activation(e[:], s_ps[:], EXP, scale=1.0 / math.sqrt(D))
-                    for g in range(GROUPS):
-                        nc.tensor.matmul(
-                            product[g][:],
-                            e[:, g * P : (g + 1) * P],
-                            v_sb[h][:, b, 0 : D + 1],
-                            start=(b == 0),
-                            stop=(b == KEY_BLOCKS - 1),
-                        )
+            for part in range(N // FW):
+                flipped = flips.tile([P, 2, FW], F32, name="flipped")
+                for i in range(FW // P):
+                    group = slice(part * FW + i * P, part * FW + (i + 1) * P)
+                    product = products.tile([P, D + 1], F32, name="product")
+                    for b0 in range(0, KEY_BLOCKS, BANK_BLOCKS):
+                        s_ps = scores.tile([P, BANK_BLOCKS, P], F32, name="s_ps")
+                        for x in range(BANK_BLOCKS):
+                            b = b0 + x
+                            nc.tensor.matmul(
+                                s_ps[:, x, :], k_sb[h][:, b * P : (b + 1) * P], q_sb[h][:, group], start=True, stop=True
+                            )
+                        e = weights.tile([P, BANK_BLOCKS, P], BF16, name="e")
+                        nc.scalar.activation(e[:], s_ps[:], EXP, scale=1.0 / math.sqrt(D))
+                        for x in range(BANK_BLOCKS):
+                            b = b0 + x
+                            nc.tensor.matmul(
+                                product[:],
+                                e[:, x, :],
+                                v_sb[h][:, b, 0 : D + 1],
+                                start=(b == 0),
+                                stop=(b == KEY_BLOCKS - 1),
+                            )
 
-                num_t = [queries_first.tile([P, D + 1], F32, name="num_t") for g in range(GROUPS)]
-                for g in range(GROUPS):
-                    nc.vector.tensor_copy(num_t[g][:], product[g][:])
+                    num_t = queries_first.tile([P, D + 1], F32, name="num_t")
+                    nc.vector.tensor_copy(num_t[:], product[:])
+                    r_t = queries_first.tile([P, 1], F32, name="r_t")
+                    nc.vector.reciprocal(r_t[:], num_t[:, D : D + 1])
+                    r_wide = queries_first.tile([P, P], F32, name="r_wide")
+                    nc.vector.tensor_copy(r_wide[:], r_t[:].to_broadcast([P, P]))
+                    nc.tensor.transpose(flipped[:, 0, i * P : (i + 1) * P], num_t[:, 0:D], identity[:])
+                    nc.tensor.transpose(flipped[:, 1, i * P : (i + 1) * P], r_wide[:], identity[:])
 
-                for part in range(JW // FW):
-                    flipped = flips.tile([P, 2, FW], F32, name="flipped")
-                    for i in range(FW // P):
-                        g = part * (FW // P) + i
-                        r_t = queries_first.tile([P, 1], F32, name="r_t")
-                        nc.vector.reciprocal(r_t[:], num_t[g][:, D : D + 1])
-                        r_wide = queries_first.tile([P, P], F32, name="r_wide")
-                        nc.vector.tensor_copy(r_wide[:], r_t[:].to_broadcast([P, P]))
-                        nc.tensor.transpose(flipped[:, 0, i * P : (i + 1) * P], num_t[g][:, 0:D], identity[:])
-                        nc.tensor.transpose(flipped[:, 1, i * P : (i + 1) * P], r_wide[:], identity[:])
-                    num_r = results.tile([P, 2, FW], F32, name="num_r")
-                    nc.vector.tensor_copy(num_r[:], flipped[:])
-                    first = (piece * JW + part * FW) // 16
-                    nc.vector.tensor_tensor(
-                        window[h][:].indirect(offsets[:, first : first + FW // 16]),
-                        num_r[:, 0, :],
-                        num_r[:, 1, :],
-                        MULT,
-                    )
+                num_r = results.tile([P, 2, FW], F32, name="num_r")
+                nc.vector.tensor_copy(num_r[:], flipped[:])
+                first = part * FW // 16
+                nc.vector.tensor_tensor(
+                    window[h][:].indirect(offsets[:, first : first + FW // 16]),
+                    num_r[:, 0, :],
+                    num_r[:, 1, :],
+                    MULT,
+                )
             nc.sync.dma_start(out[h * D : (h + 1) * D, :], window[h][:])

@@ -7,8 +7,10 @@ H, D, S, T, N = 4, 128, 2048, 2048, 1024
 P = 128
 KEY_BLOCKS = T // P
 BANK_BLOCKS = 4
-VW = 144
-FW = 256
+QUERY_GROUPS = N // P
+PAIR = 2
+AHEAD = 3
+V_PITCH = 144
 
 FLOPS = 4 * H * D * T * N
 
@@ -22,10 +24,10 @@ def tile_longcontextattention_b_kernel(tc, base, q, k, v, offs, out):
     v_blocks = v.rearrange("(b p) c -> p b c", p=P)
     with (
         tc.tile_pool(name="held", bufs=1) as held,
-        tc.tile_pool(name="weights", bufs=6) as weights,
-        tc.tile_pool(name="queries_first", bufs=4) as queries_first,
-        tc.tile_pool(name="results", bufs=2) as results,
-        tc.psum_pool(name="scores", bufs=4) as scores,
+        tc.tile_pool(name="exps", bufs=2 * (AHEAD + 1)) as exps,
+        tc.tile_pool(name="queries_first", bufs=2) as queries_first,
+        tc.tile_pool(name="channels_first", bufs=2) as channels_first,
+        tc.psum_pool(name="scores", bufs=AHEAD + 1) as scores,
         tc.psum_pool(name="products", bufs=3) as products,
         tc.psum_pool(name="flips", bufs=1) as flips,
     ):
@@ -36,9 +38,9 @@ def tile_longcontextattention_b_kernel(tc, base, q, k, v, offs, out):
             rows = slice(h * D, (h + 1) * D)
             q_sb.append(held.tile([P, N], BF16, name="q%d" % h))
             k_sb.append(held.tile([P, T], BF16, name="k%d" % h))
-            v_sb.append(held.tile([P, KEY_BLOCKS, VW], BF16, name="v%d" % h))
+            v_sb.append(held.tile([P, KEY_BLOCKS, V_PITCH], BF16, name="v%d" % h))
             window.append(held.tile([P, S], F32, name="window%d" % h))
-            nc.gpsimd.memset(v_sb[h][:, :, D:VW], 1.0)
+            nc.gpsimd.memset(v_sb[h][:, :, D:V_PITCH], 1.0)
             nc.sync.dma_start(q_sb[h][:], q[rows, :])
             for c0 in range(0, T, BANK_BLOCKS * P):
                 nc.sync.dma_start(k_sb[h][:, c0 : c0 + BANK_BLOCKS * P], k[rows, c0 : c0 + BANK_BLOCKS * P])
@@ -50,47 +52,58 @@ def tile_longcontextattention_b_kernel(tc, base, q, k, v, offs, out):
         identity = held.tile([P, P], F32, name="identity")
         make_identity(nc, identity[:])
 
-        for h in range(H):
-            for part in range(N // FW):
-                flipped = flips.tile([P, 2, FW], F32, name="flipped")
-                for i in range(FW // P):
-                    group = slice(part * FW + i * P, part * FW + (i + 1) * P)
-                    product = products.tile([P, D + 1], F32, name="product")
-                    for b0 in range(0, KEY_BLOCKS, BANK_BLOCKS):
-                        s_ps = scores.tile([P, BANK_BLOCKS, P], F32, name="s_ps")
-                        for x in range(BANK_BLOCKS):
-                            b = b0 + x
-                            nc.tensor.matmul(
-                                s_ps[:, x, :], k_sb[h][:, b * P : (b + 1) * P], q_sb[h][:, group], start=True, stop=True
-                            )
-                        e = weights.tile([P, BANK_BLOCKS, P], BF16, name="e")
-                        nc.scalar.activation(e[:], s_ps[:], EXP, scale=1.0 / math.sqrt(D))
-                        for x in range(BANK_BLOCKS):
-                            b = b0 + x
-                            nc.tensor.matmul(
-                                product[:],
-                                e[:, x, :],
-                                v_sb[h][:, b, 0 : D + 1],
-                                start=(b == 0),
-                                stop=(b == KEY_BLOCKS - 1),
-                            )
-
-                    num_t = queries_first.tile([P, D + 1], F32, name="num_t")
-                    nc.vector.tensor_copy(num_t[:], product[:])
-                    r_t = queries_first.tile([P, 1], F32, name="r_t")
-                    nc.vector.reciprocal(r_t[:], num_t[:, D : D + 1])
-                    r_wide = queries_first.tile([P, P], F32, name="r_wide")
-                    nc.vector.tensor_copy(r_wide[:], r_t[:].to_broadcast([P, P]))
-                    nc.tensor.transpose(flipped[:, 0, i * P : (i + 1) * P], num_t[:, 0:D], identity[:])
-                    nc.tensor.transpose(flipped[:, 1, i * P : (i + 1) * P], r_wide[:], identity[:])
-
-                num_r = results.tile([P, 2, FW], F32, name="num_r")
-                nc.vector.tensor_copy(num_r[:], flipped[:])
-                first = part * FW // 16
-                nc.vector.tensor_tensor(
-                    window[h][:].indirect(offsets[:, first : first + FW // 16]),
-                    num_r[:, 0, :],
-                    num_r[:, 1, :],
-                    MULT,
+        def scores_of(h, g, b0):
+            s_ps = scores.tile([P, BANK_BLOCKS, P], F32, name="s_ps")
+            for x in range(BANK_BLOCKS):
+                b = b0 + x
+                nc.tensor.matmul(
+                    s_ps[:, x, :], k_sb[h][:, b * P : (b + 1) * P], q_sb[h][:, g * P : (g + 1) * P], start=True, stop=True
                 )
-            nc.sync.dma_start(out[h * D : (h + 1) * D, :], window[h][:])
+            return s_ps
+
+        def place(h, g, num_t, r_wide):
+            flipped = flips.tile([P, 2, PAIR * P], F32, name="flipped")
+            for i in range(PAIR):
+                nc.tensor.transpose(flipped[:, 0, i * P : (i + 1) * P], num_t[:, i, 0:D], identity[:])
+                nc.tensor.transpose(flipped[:, 1, i * P : (i + 1) * P], r_wide[:, i, :], identity[:])
+            num_r = channels_first.tile([P, 2, PAIR * P], F32, name="num_r")
+            nc.vector.tensor_copy(num_r[:], flipped[:])
+            stop = (g + 1) * P // 16
+            nc.vector.tensor_tensor(
+                window[h][:].indirect(offsets[:, stop - PAIR * P // 16 : stop]), num_r[:, 0, :], num_r[:, 1, :], MULT
+            )
+            if g == QUERY_GROUPS - 1:
+                nc.sync.dma_start(out[h * D : (h + 1) * D, :], window[h][:])
+
+        steps = [(h, g, b0) for h in range(H) for g in range(QUERY_GROUPS) for b0 in range(0, KEY_BLOCKS, BANK_BLOCKS)]
+        score_tiles = [scores_of(*step) for step in steps[:AHEAD]]
+        complete = None
+        for n, (h, g, b0) in enumerate(steps):
+            if n + AHEAD < len(steps):
+                score_tiles.append(scores_of(*steps[n + AHEAD]))
+            e = exps.tile([P, BANK_BLOCKS, P], BF16, name="e")
+            nc.scalar.activation(e[:], score_tiles[n][:], EXP, scale=1.0 / math.sqrt(D))
+
+            if b0 == 0:
+                product = products.tile([P, D + 1], F32, name="product")
+            for x in range(BANK_BLOCKS):
+                b = b0 + x
+                nc.tensor.matmul(
+                    product[:], e[:, x, :], v_sb[h][:, b, 0 : D + 1], start=(b == 0), stop=(b == KEY_BLOCKS - 1)
+                )
+            if b0 + BANK_BLOCKS < KEY_BLOCKS:
+                continue
+
+            i = g % PAIR
+            if i == 0:
+                num_t = queries_first.tile([P, PAIR, D + 1], F32, name="num_t")
+            nc.vector.tensor_copy(num_t[:, i, :], product[:])
+            if i == 0 and complete:
+                place(*complete)
+            if i == PAIR - 1:
+                r_t = queries_first.tile([P, PAIR, 1], F32, name="r_t")
+                nc.vector.reciprocal(r_t[:], num_t[:, :, D : D + 1])
+                r_wide = queries_first.tile([P, PAIR, P], F32, name="r_wide")
+                nc.vector.tensor_copy(r_wide[:], r_t[:].to_broadcast([P, PAIR, P]))
+                complete = (h, g, num_t, r_wide)
+        place(*complete)

@@ -6,10 +6,11 @@ from concourse.masks import make_identity
 H, D, S, T, N = 4, 128, 2048, 2048, 1024
 P = 128
 KEY_BLOCKS = T // P
-BANK_BLOCKS = 4
-QUERY_GROUPS = N // P
 PAIR = 2
-AHEAD = 3
+STEP_BLOCKS = 2
+PAIRS = N // (PAIR * P)
+AHEAD = 2
+PLACE_LATE = 3
 V_PITCH = 144
 
 FLOPS = 4 * H * D * T * N
@@ -28,82 +29,101 @@ def tile_longcontextattention_b_kernel(tc, base, q, k, v, offs, out):
         tc.tile_pool(name="queries_first", bufs=2) as queries_first,
         tc.tile_pool(name="channels_first", bufs=2) as channels_first,
         tc.psum_pool(name="scores", bufs=AHEAD + 1) as scores,
-        tc.psum_pool(name="products", bufs=3) as products,
+        tc.psum_pool(name="products", bufs=2) as products,
         tc.psum_pool(name="flips", bufs=1) as flips,
     ):
         offsets = held.tile([P, N // 16], U16, name="offsets")
 
         q_sb, k_sb, v_sb, window = [], [], [], []
         for h in range(H):
-            rows = slice(h * D, (h + 1) * D)
             q_sb.append(held.tile([P, N], BF16, name="q%d" % h))
             k_sb.append(held.tile([P, T], BF16, name="k%d" % h))
             v_sb.append(held.tile([P, KEY_BLOCKS, V_PITCH], BF16, name="v%d" % h))
             window.append(held.tile([P, S], F32, name="window%d" % h))
+
+        quarter, half = T // 4, T // 2
+        nc.gpsimd.memset(v_sb[0][:, :, D:V_PITCH], 1.0)
+        nc.sync.dma_start(k_sb[0][:, 0:quarter], k[0:D, 0:quarter])
+        nc.scalar.dma_start(q_sb[0][:, 0 : PAIR * P], q[0:D, 0 : PAIR * P])
+        nc.sync.dma_start(k_sb[0][:, quarter:half], k[0:D, quarter:half])
+        nc.scalar.dma_start(v_sb[0][:, 0 : KEY_BLOCKS // 2, 0:D], v_blocks[:, 0 : KEY_BLOCKS // 2, 0:D])
+        nc.sync.dma_start(k_sb[0][:, half:T], k[0:D, half:T])
+        nc.sync.dma_start(v_sb[0][:, KEY_BLOCKS // 2 : KEY_BLOCKS, 0:D], v_blocks[:, KEY_BLOCKS // 2 : KEY_BLOCKS, 0:D])
+        nc.sync.dma_start(q_sb[0][:, PAIR * P : N], q[0:D, PAIR * P : N])
+        nc.sync.dma_start(offsets[:], offs)
+        nc.sync.dma_start(window[0][:], base[0:D, :])
+        for h in range(1, H):
+            rows = slice(h * D, (h + 1) * D)
             nc.gpsimd.memset(v_sb[h][:, :, D:V_PITCH], 1.0)
             nc.sync.dma_start(q_sb[h][:], q[rows, :])
-            for c0 in range(0, T, BANK_BLOCKS * P):
-                nc.sync.dma_start(k_sb[h][:, c0 : c0 + BANK_BLOCKS * P], k[rows, c0 : c0 + BANK_BLOCKS * P])
+            nc.sync.dma_start(k_sb[h][:], k[rows, :])
             nc.sync.dma_start(v_sb[h][:, :, 0:D], v_blocks[:, :, rows])
-            if h == 0:
-                nc.sync.dma_start(offsets[:], offs)
             nc.sync.dma_start(window[h][:], base[rows, :])
 
         identity = held.tile([P, P], F32, name="identity")
         make_identity(nc, identity[:])
 
-        def scores_of(h, g, b0):
-            s_ps = scores.tile([P, BANK_BLOCKS, P], F32, name="s_ps")
-            for x in range(BANK_BLOCKS):
+        def scores_of(h, pair, b0):
+            s_ps = scores.tile([P, STEP_BLOCKS, PAIR * P], F32, name="s_ps")
+            for x in range(STEP_BLOCKS):
                 b = b0 + x
                 nc.tensor.matmul(
-                    s_ps[:, x, :], k_sb[h][:, b * P : (b + 1) * P], q_sb[h][:, g * P : (g + 1) * P], start=True, stop=True
+                    s_ps[:, x, :],
+                    k_sb[h][:, b * P : (b + 1) * P],
+                    q_sb[h][:, pair * PAIR * P : (pair + 1) * PAIR * P],
+                    start=True,
+                    stop=True,
                 )
             return s_ps
 
-        def place(h, g, num_t, r_wide):
+        def place(h, pair, num_t, r_wide):
             flipped = flips.tile([P, 2, PAIR * P], F32, name="flipped")
             for i in range(PAIR):
                 nc.tensor.transpose(flipped[:, 0, i * P : (i + 1) * P], num_t[:, i, 0:D], identity[:])
                 nc.tensor.transpose(flipped[:, 1, i * P : (i + 1) * P], r_wide[:, i, :], identity[:])
             num_r = channels_first.tile([P, 2, PAIR * P], F32, name="num_r")
             nc.vector.tensor_copy(num_r[:], flipped[:])
-            stop = (g + 1) * P // 16
+            columns = PAIR * P // 16
             nc.vector.tensor_tensor(
-                window[h][:].indirect(offsets[:, stop - PAIR * P // 16 : stop]), num_r[:, 0, :], num_r[:, 1, :], MULT
+                window[h][:].indirect(offsets[:, pair * columns : (pair + 1) * columns]),
+                num_r[:, 0, :],
+                num_r[:, 1, :],
+                MULT,
             )
-            if g == QUERY_GROUPS - 1:
+            if pair == PAIRS - 1:
                 nc.sync.dma_start(out[h * D : (h + 1) * D, :], window[h][:])
 
-        steps = [(h, g, b0) for h in range(H) for g in range(QUERY_GROUPS) for b0 in range(0, KEY_BLOCKS, BANK_BLOCKS)]
+        steps = [(h, pair, b0) for h in range(H) for pair in range(PAIRS) for b0 in range(0, KEY_BLOCKS, STEP_BLOCKS)]
         score_tiles = [scores_of(*step) for step in steps[:AHEAD]]
         complete = None
-        for n, (h, g, b0) in enumerate(steps):
+        for n, (h, pair, b0) in enumerate(steps):
             if n + AHEAD < len(steps):
                 score_tiles.append(scores_of(*steps[n + AHEAD]))
-            e = exps.tile([P, BANK_BLOCKS, P], BF16, name="e")
+            e = exps.tile([P, STEP_BLOCKS, PAIR * P], BF16, name="e")
             nc.scalar.activation(e[:], score_tiles[n][:], EXP, scale=1.0 / math.sqrt(D))
 
             if b0 == 0:
-                product = products.tile([P, D + 1], F32, name="product")
-            for x in range(BANK_BLOCKS):
+                product = [products.tile([P, D + 1], F32, name="product%d" % i) for i in range(PAIR)]
+            for x in range(STEP_BLOCKS):
                 b = b0 + x
-                nc.tensor.matmul(
-                    product[:], e[:, x, :], v_sb[h][:, b, 0 : D + 1], start=(b == 0), stop=(b == KEY_BLOCKS - 1)
-                )
-            if b0 + BANK_BLOCKS < KEY_BLOCKS:
-                continue
+                for i in range(PAIR):
+                    nc.tensor.matmul(
+                        product[i][:],
+                        e[:, x, i * P : (i + 1) * P],
+                        v_sb[h][:, b, 0 : D + 1],
+                        start=(b == 0),
+                        stop=(b == KEY_BLOCKS - 1),
+                    )
 
-            i = g % PAIR
-            if i == 0:
-                num_t = queries_first.tile([P, PAIR, D + 1], F32, name="num_t")
-            nc.vector.tensor_copy(num_t[:, i, :], product[:])
-            if i == 0 and complete:
+            if b0 == (PLACE_LATE - 1) * STEP_BLOCKS and complete:
                 place(*complete)
-            if i == PAIR - 1:
+            if b0 + STEP_BLOCKS == KEY_BLOCKS:
+                num_t = queries_first.tile([P, PAIR, D + 1], F32, name="num_t")
+                for i in range(PAIR):
+                    nc.vector.tensor_copy(num_t[:, i, :], product[i][:])
                 r_t = queries_first.tile([P, PAIR, 1], F32, name="r_t")
                 nc.vector.reciprocal(r_t[:], num_t[:, :, D : D + 1])
                 r_wide = queries_first.tile([P, PAIR, P], F32, name="r_wide")
                 nc.vector.tensor_copy(r_wide[:], r_t[:].to_broadcast([P, PAIR, P]))
-                complete = (h, g, num_t, r_wide)
+                complete = (h, pair, num_t, r_wide)
         place(*complete)

@@ -9,7 +9,7 @@ KEY_BLOCKS = T // P
 PAIR = 2
 STEP_BLOCKS = 2
 PAIRS = N // (PAIR * P)
-AHEAD = 2
+AHEAD = 3
 PLACE_LATE = 3
 V_PITCH = 144
 
@@ -30,7 +30,7 @@ def tile_longcontextattention_b_kernel(tc, base, q, k, v, offs, out):
         tc.tile_pool(name="channels_first", bufs=2) as channels_first,
         tc.psum_pool(name="scores", bufs=AHEAD + 1) as scores,
         tc.psum_pool(name="products", bufs=2) as products,
-        tc.psum_pool(name="flips", bufs=1) as flips,
+        tc.psum_pool(name="flips", bufs=2) as flips,
     ):
         offsets = held.tile([P, N // 16], U16, name="offsets")
 
@@ -76,11 +76,11 @@ def tile_longcontextattention_b_kernel(tc, base, q, k, v, offs, out):
                 )
             return s_ps
 
-        def place(h, pair, num_t, r_wide):
+        def place(h, pair, num_t, r_t):
             flipped = flips.tile([P, 2, PAIR * P], F32, name="flipped")
             for i in range(PAIR):
-                nc.tensor.transpose(flipped[:, 0, i * P : (i + 1) * P], num_t[:, i, 0:D], identity[:])
-                nc.tensor.transpose(flipped[:, 1, i * P : (i + 1) * P], r_wide[:, i, :], identity[:])
+                nc.tensor.transpose(flipped[:, 0, i * P : (i + 1) * P], num_t[:, i, :], identity[:])
+                nc.tensor.transpose(flipped[:, 1, i * P : (i + 1) * P], r_t[:, i, :].to_broadcast([P, P]), identity[:])
             num_r = channels_first.tile([P, 2, PAIR * P], F32, name="num_r")
             nc.vector.tensor_copy(num_r[:], flipped[:])
             columns = PAIR * P // 16
@@ -103,27 +103,24 @@ def tile_longcontextattention_b_kernel(tc, base, q, k, v, offs, out):
             nc.scalar.activation(e[:], score_tiles[n][:], EXP, scale=1.0 / math.sqrt(D))
 
             if b0 == 0:
-                product = [products.tile([P, D + 1], F32, name="product%d" % i) for i in range(PAIR)]
+                product = products.tile([P, PAIR, D + 1], F32, name="product")
             for x in range(STEP_BLOCKS):
                 b = b0 + x
                 for i in range(PAIR):
                     nc.tensor.matmul(
-                        product[i][:],
+                        product[:, i, :],
                         e[:, x, i * P : (i + 1) * P],
                         v_sb[h][:, b, 0 : D + 1],
-                        start=(b == 0),
-                        stop=(b == KEY_BLOCKS - 1),
+                        start=(b == 0 and i == 0),
+                        stop=(b == KEY_BLOCKS - 1 and i == PAIR - 1),
                     )
 
             if b0 == (PLACE_LATE - 1) * STEP_BLOCKS and complete:
                 place(*complete)
             if b0 + STEP_BLOCKS == KEY_BLOCKS:
-                num_t = queries_first.tile([P, PAIR, D + 1], F32, name="num_t")
-                for i in range(PAIR):
-                    nc.vector.tensor_copy(num_t[:, i, :], product[i][:])
                 r_t = queries_first.tile([P, PAIR, 1], F32, name="r_t")
-                nc.vector.reciprocal(r_t[:], num_t[:, :, D : D + 1])
-                r_wide = queries_first.tile([P, PAIR, P], F32, name="r_wide")
-                nc.vector.tensor_copy(r_wide[:], r_t[:].to_broadcast([P, PAIR, P]))
-                complete = (h, pair, num_t, r_wide)
+                nc.vector.reciprocal(r_t[:], product[:, :, D : D + 1])
+                num_t = queries_first.tile([P, PAIR, D], F32, name="num_t")
+                nc.vector.tensor_copy(num_t[:], product[:, :, 0:D])
+                complete = (h, pair, num_t, r_t)
         place(*complete)

@@ -10,7 +10,7 @@ PAIR = 2
 STEP_BLOCKS = 2
 PAIRS = N // (PAIR * P)
 AHEAD = 3
-PLACE_LATE = 3
+PLACE_LATE = 2
 V_PITCH = 144
 
 FLOPS = 4 * H * D * T * N

@@ -30,7 +30,7 @@ def tile_longcontextattention_b_kernel(tc, base, q, k, v, offs, out):
         tc.tile_pool(name="channels_first", bufs=2) as channels_first,
         tc.psum_pool(name="scores", bufs=AHEAD + 1) as scores,
         tc.psum_pool(name="products", bufs=2) as products,
-        tc.psum_pool(name="flips", bufs=2) as flips,
+        tc.psum_pool(name="flips", bufs=1) as flips,
     ):
         offsets = held.tile([P, N // 16], U16, name="offsets")
 
@@ -77,18 +77,19 @@ def tile_longcontextattention_b_kernel(tc, base, q, k, v, offs, out):
             return s_ps
 
         def place(h, pair, num_t, r_t):
-            flipped = flips.tile([P, 2, PAIR * P], F32, name="flipped")
+            r_ps = flips.tile([P, PAIR * P], F32, name="r_ps")
             for i in range(PAIR):
-                nc.tensor.transpose(flipped[:, 0, i * P : (i + 1) * P], num_t[:, i, :], identity[:])
-                nc.tensor.transpose(flipped[:, 1, i * P : (i + 1) * P], r_t[:, i, :].to_broadcast([P, P]), identity[:])
-            num_r = channels_first.tile([P, 2, PAIR * P], F32, name="num_r")
-            nc.vector.tensor_copy(num_r[:], flipped[:])
+                nc.tensor.transpose(r_ps[:, i * P : (i + 1) * P], r_t[:, i, :].to_broadcast([P, P]), identity[:])
+            num_ps = flips.tile([P, PAIR * P], F32, name="num_ps")
+            for i in range(PAIR):
+                nc.tensor.transpose(num_ps[:, i * P : (i + 1) * P], num_t[:, i, :], identity[:])
+            r_sb = channels_first.tile([P, PAIR * P], F32, name="r_sb")
+            nc.vector.tensor_copy(r_sb[:], r_ps[:])
+            num_sb = channels_first.tile([P, PAIR * P], F32, name="num_sb")
+            nc.vector.tensor_copy(num_sb[:], num_ps[:])
             columns = PAIR * P // 16
             nc.vector.tensor_tensor(
-                window[h][:].indirect(offsets[:, pair * columns : (pair + 1) * columns]),
-                num_r[:, 0, :],
-                num_r[:, 1, :],
-                MULT,
+                window[h][:].indirect(offsets[:, pair * columns : (pair + 1) * columns]), num_sb[:], r_sb[:], MULT
             )
             if pair == PAIRS - 1:
                 nc.sync.dma_start(out[h * D : (h + 1) * D, :], window[h][:])

@@ -10,7 +10,8 @@ PAIR = 2
 STEP_BLOCKS = 2
 PAIRS = N // (PAIR * P)
 AHEAD = 3
-PLACE_LATE = 2
+FLIPS = 2 * PAIR
+FLIP_LATE = 1
 V_PITCH = 144
 
 FLOPS = 4 * H * D * T * N
@@ -76,13 +77,7 @@ def tile_longcontextattention_b_kernel(tc, base, q, k, v, offs, out):
                 )
             return s_ps
 
-        def place(h, pair, num_t, r_t):
-            r_ps = flips.tile([P, PAIR * P], F32, name="r_ps")
-            for i in range(PAIR):
-                nc.tensor.transpose(r_ps[:, i * P : (i + 1) * P], r_t[:, i, :].to_broadcast([P, P]), identity[:])
-            num_ps = flips.tile([P, PAIR * P], F32, name="num_ps")
-            for i in range(PAIR):
-                nc.tensor.transpose(num_ps[:, i * P : (i + 1) * P], num_t[:, i, :], identity[:])
+        def place(h, pair, num_ps, r_ps):
             r_sb = channels_first.tile([P, PAIR * P], F32, name="r_sb")
             nc.vector.tensor_copy(r_sb[:], r_ps[:])
             num_sb = channels_first.tile([P, PAIR * P], F32, name="num_sb")
@@ -94,12 +89,26 @@ def tile_longcontextattention_b_kernel(tc, base, q, k, v, offs, out):
             if pair == PAIRS - 1:
                 nc.sync.dma_start(out[h * D : (h + 1) * D, :], window[h][:])
 
+        def flip(number, h, pair, num_t, r_t, num_ps, r_ps):
+            i = number % PAIR
+            columns = slice(i * P, (i + 1) * P)
+            if number < PAIR:
+                nc.tensor.transpose(r_ps[:, columns], r_t[:, i, :].to_broadcast([P, P]), identity[:])
+            else:
+                nc.tensor.transpose(num_ps[:, columns], num_t[:, i, :], identity[:])
+            if number == FLIPS - 1:
+                place(h, pair, num_ps, r_ps)
+
         steps = [(h, pair, b0) for h in range(H) for pair in range(PAIRS) for b0 in range(0, KEY_BLOCKS, STEP_BLOCKS)]
         score_tiles = [scores_of(*step) for step in steps[:AHEAD]]
         complete = None
         for n, (h, pair, b0) in enumerate(steps):
             if n + AHEAD < len(steps):
                 score_tiles.append(scores_of(*steps[n + AHEAD]))
+            number = 2 * (b0 // STEP_BLOCKS - FLIP_LATE)
+            flipping = complete and 0 <= number < FLIPS
+            if flipping:
+                flip(number, *complete)
             e = exps.tile([P, STEP_BLOCKS, PAIR * P], BF16, name="e")
             nc.scalar.activation(e[:], score_tiles[n][:], EXP, scale=1.0 / math.sqrt(D))
 
@@ -116,12 +125,15 @@ def tile_longcontextattention_b_kernel(tc, base, q, k, v, offs, out):
                         stop=(b == KEY_BLOCKS - 1 and i == PAIR - 1),
                     )
 
-            if b0 == (PLACE_LATE - 1) * STEP_BLOCKS and complete:
-                place(*complete)
+            if flipping:
+                flip(number + 1, *complete)
             if b0 + STEP_BLOCKS == KEY_BLOCKS:
                 r_t = queries_first.tile([P, PAIR, 1], F32, name="r_t")
                 nc.vector.reciprocal(r_t[:], product[:, :, D : D + 1])
                 num_t = queries_first.tile([P, PAIR, D], F32, name="num_t")
                 nc.vector.tensor_copy(num_t[:], product[:, :, 0:D])
-                complete = (h, pair, num_t, r_t)
-        place(*complete)
+                r_ps = flips.tile([P, PAIR * P], F32, name="r_ps")
+                num_ps = flips.tile([P, PAIR * P], F32, name="num_ps")
+                complete = (h, pair, num_t, r_t, num_ps, r_ps)
+        for number in range(FLIPS):
+            flip(number, *complete)

@@ -64,18 +64,15 @@ def tile_longcontextattention_b_kernel(tc, base, q, k, v, offs, out):
         identity = held.tile([P, P], F32, name="identity")
         make_identity(nc, identity[:])
 
-        def scores_of(h, pair, b0):
-            s_ps = scores.tile([P, STEP_BLOCKS, PAIR * P], F32, name="s_ps")
-            for x in range(STEP_BLOCKS):
-                b = b0 + x
-                nc.tensor.matmul(
-                    s_ps[:, x, :],
-                    k_sb[h][:, b * P : (b + 1) * P],
-                    q_sb[h][:, pair * PAIR * P : (pair + 1) * PAIR * P],
-                    start=True,
-                    stop=True,
-                )
-            return s_ps
+        def score(s_ps, x, h, pair, b0):
+            b = b0 + x
+            nc.tensor.matmul(
+                s_ps[:, x, :],
+                k_sb[h][:, b * P : (b + 1) * P],
+                q_sb[h][:, pair * PAIR * P : (pair + 1) * PAIR * P],
+                start=True,
+                stop=True,
+            )
 
         def place(h, pair, num_ps, r_ps):
             r_sb = channels_first.tile([P, PAIR * P], F32, name="r_sb")
@@ -100,21 +97,28 @@ def tile_longcontextattention_b_kernel(tc, base, q, k, v, offs, out):
                 place(h, pair, num_ps, r_ps)
 
         steps = [(h, pair, b0) for h in range(H) for pair in range(PAIRS) for b0 in range(0, KEY_BLOCKS, STEP_BLOCKS)]
-        score_tiles = [scores_of(*step) for step in steps[:AHEAD]]
+        score_tiles = []
+        for step in steps[:AHEAD]:
+            score_tiles.append(scores.tile([P, STEP_BLOCKS, PAIR * P], F32, name="s_ps"))
+            for x in range(STEP_BLOCKS):
+                score(score_tiles[-1], x, *step)
         complete = None
         for n, (h, pair, b0) in enumerate(steps):
-            if n + AHEAD < len(steps):
-                score_tiles.append(scores_of(*steps[n + AHEAD]))
-            number = 2 * (b0 // STEP_BLOCKS - FLIP_LATE)
-            flipping = complete and 0 <= number < FLIPS
-            if flipping:
-                flip(number, *complete)
             e = exps.tile([P, STEP_BLOCKS, PAIR * P], BF16, name="e")
             nc.scalar.activation(e[:], score_tiles[n][:], EXP, scale=1.0 / math.sqrt(D))
 
+            ahead = steps[n + AHEAD] if n + AHEAD < len(steps) else None
+            if ahead:
+                score_tiles.append(scores.tile([P, STEP_BLOCKS, PAIR * P], F32, name="s_ps"))
+            number = STEP_BLOCKS * (b0 // STEP_BLOCKS - FLIP_LATE)
+            flipping = complete and 0 <= number < FLIPS
             if b0 == 0:
                 product = products.tile([P, PAIR, D + 1], F32, name="product")
             for x in range(STEP_BLOCKS):
+                if ahead:
+                    score(score_tiles[-1], x, *ahead)
+                if flipping:
+                    flip(number + x, *complete)
                 b = b0 + x
                 for i in range(PAIR):
                     nc.tensor.matmul(
@@ -125,8 +129,6 @@ def tile_longcontextattention_b_kernel(tc, base, q, k, v, offs, out):
                         stop=(b == KEY_BLOCKS - 1 and i == PAIR - 1),
                     )
 
-            if flipping:
-                flip(number + 1, *complete)
             if b0 + STEP_BLOCKS == KEY_BLOCKS:
                 r_t = queries_first.tile([P, PAIR, 1], F32, name="r_t")
                 nc.vector.reciprocal(r_t[:], product[:, :, D : D + 1])

@@ -96,16 +96,22 @@ def tile_longcontextattention_b_kernel(tc, base, q, k, v, offs, out):
             if number == FLIPS - 1:
                 place(h, pair, num_ps, r_ps)
 
-        steps = [(h, pair, b0) for h in range(H) for pair in range(PAIRS) for b0 in range(0, KEY_BLOCKS, STEP_BLOCKS)]
+        def halves(h, pair, b0, blocks):
+            return [(h, pair, b0, 1), (h, pair, b0 + 1, 1)]
+
+        steps = [
+            (h, pair, b0, STEP_BLOCKS) for h in range(H) for pair in range(PAIRS) for b0 in range(0, KEY_BLOCKS, STEP_BLOCKS)
+        ]
+        steps = halves(*steps[0]) + steps[1:-1] + halves(*steps[-1])
         score_tiles = []
-        for step in steps[:AHEAD]:
+        for h, pair, b0, blocks in steps[:AHEAD]:
             score_tiles.append(scores.tile([P, STEP_BLOCKS, PAIR * P], F32, name="s_ps"))
-            for x in range(STEP_BLOCKS):
-                score(score_tiles[-1], x, *step)
+            for x in range(blocks):
+                score(score_tiles[-1], x, h, pair, b0)
         complete = None
-        for n, (h, pair, b0) in enumerate(steps):
+        for n, (h, pair, b0, blocks) in enumerate(steps):
             e = exps.tile([P, STEP_BLOCKS, PAIR * P], BF16, name="e")
-            nc.scalar.activation(e[:], score_tiles[n][:], EXP, scale=1.0 / math.sqrt(D))
+            nc.scalar.activation(e[:, 0:blocks, :], score_tiles[n][:, 0:blocks, :], EXP, scale=1.0 / math.sqrt(D))
 
             ahead = steps[n + AHEAD] if n + AHEAD < len(steps) else None
             if ahead:
@@ -115,10 +121,12 @@ def tile_longcontextattention_b_kernel(tc, base, q, k, v, offs, out):
             if b0 == 0:
                 product = products.tile([P, PAIR, D + 1], F32, name="product")
             for x in range(STEP_BLOCKS):
-                if ahead:
-                    score(score_tiles[-1], x, *ahead)
+                if ahead and x < ahead[3]:
+                    score(score_tiles[-1], x, *ahead[:3])
                 if flipping:
                     flip(number + x, *complete)
+                if x >= blocks:
+                    continue
                 b = b0 + x
                 for i in range(PAIR):
                     nc.tensor.matmul(
@@ -129,7 +137,7 @@ def tile_longcontextattention_b_kernel(tc, base, q, k, v, offs, out):
                         stop=(b == KEY_BLOCKS - 1 and i == PAIR - 1),
                     )
 
-            if b0 + STEP_BLOCKS == KEY_BLOCKS:
+            if b0 + blocks == KEY_BLOCKS:
                 r_t = queries_first.tile([P, PAIR, 1], F32, name="r_t")
                 nc.vector.reciprocal(r_t[:], product[:, :, D : D + 1])
                 num_t = queries_first.tile([P, PAIR, D], F32, name="num_t")

@@ -12,7 +12,8 @@ PAIRS = N // (PAIR * P)
 AHEAD = 3
 FLIPS = 2 * PAIR
 FLIP_LATE = 1
-V_PITCH = 144
+V_PITCH = 256
+V_USED = 144
 
 FLOPS = 4 * H * D * T * N
 
@@ -43,11 +44,14 @@ def tile_longcontextattention_b_kernel(tc, base, q, k, v, offs, out):
             window.append(held.tile([P, S], F32, name="window%d" % h))
 
         quarter, half = T // 4, T // 2
-        nc.gpsimd.memset(v_sb[0][:, :, D:V_PITCH], 1.0)
+        nc.gpsimd.memset(v_sb[0][:, :, D:V_USED], 1.0)
         nc.sync.dma_start(k_sb[0][:, 0:quarter], k[0:D, 0:quarter])
         nc.scalar.dma_start(q_sb[0][:, 0 : PAIR * P], q[0:D, 0 : PAIR * P])
         nc.sync.dma_start(k_sb[0][:, quarter:half], k[0:D, quarter:half])
-        nc.scalar.dma_start(v_sb[0][:, 0 : KEY_BLOCKS // 2, 0:D], v_blocks[:, 0 : KEY_BLOCKS // 2, 0:D])
+        nc.scalar.dma_start(v_sb[0][:, 0 : KEY_BLOCKS // 4, 0:D], v_blocks[:, 0 : KEY_BLOCKS // 4, 0:D])
+        nc.sync.dma_start(
+            v_sb[0][:, KEY_BLOCKS // 4 : KEY_BLOCKS // 2, 0:D], v_blocks[:, KEY_BLOCKS // 4 : KEY_BLOCKS // 2, 0:D]
+        )
         nc.sync.dma_start(k_sb[0][:, half:T], k[0:D, half:T])
         nc.sync.dma_start(v_sb[0][:, KEY_BLOCKS // 2 : KEY_BLOCKS, 0:D], v_blocks[:, KEY_BLOCKS // 2 : KEY_BLOCKS, 0:D])
         nc.sync.dma_start(q_sb[0][:, PAIR * P : N], q[0:D, PAIR * P : N])
@@ -55,7 +59,7 @@ def tile_longcontextattention_b_kernel(tc, base, q, k, v, offs, out):
         nc.sync.dma_start(window[0][:], base[0:D, :])
         for h in range(1, H):
             rows = slice(h * D, (h + 1) * D)
-            nc.gpsimd.memset(v_sb[h][:, :, D:V_PITCH], 1.0)
+            nc.gpsimd.memset(v_sb[h][:, :, D:V_USED], 1.0)
             nc.sync.dma_start(q_sb[h][:], q[rows, :])
             nc.sync.dma_start(k_sb[h][:], k[rows, :])
             nc.sync.dma_start(v_sb[h][:, :, 0:D], v_blocks[:, :, rows])

@@ -27,6 +27,7 @@ def tile_longcontextattention_b_kernel(tc, base, q, k, v, offs, out):
     v_blocks = v.rearrange("(b p) c -> p b c", p=P)
     with (
         tc.tile_pool(name="held", bufs=1) as held,
+        tc.tile_pool(name="inputs", bufs=2) as inputs,
         tc.tile_pool(name="exps", bufs=2 * (AHEAD + 1)) as exps,
         tc.tile_pool(name="queries_first", bufs=2) as queries_first,
         tc.tile_pool(name="channels_first", bufs=2) as channels_first,
@@ -37,11 +38,14 @@ def tile_longcontextattention_b_kernel(tc, base, q, k, v, offs, out):
         offsets = held.tile([P, N // 16], U16, name="offsets")
 
         q_sb, k_sb, v_sb, window = [], [], [], []
-        for h in range(H):
-            q_sb.append(held.tile([P, N], BF16, name="q%d" % h))
-            k_sb.append(held.tile([P, T], BF16, name="k%d" % h))
-            v_sb.append(held.tile([P, KEY_BLOCKS, V_PITCH], BF16, name="v%d" % h))
-            window.append(held.tile([P, S], F32, name="window%d" % h))
+
+        def allocate():
+            q_sb.append(inputs.tile([P, N], BF16, name="q"))
+            k_sb.append(inputs.tile([P, T], BF16, name="k"))
+            v_sb.append(inputs.tile([P, KEY_BLOCKS, V_PITCH], BF16, name="v"))
+            window.append(inputs.tile([P, S], F32, name="window"))
+
+        allocate()
 
         quarter, half = T // 4, T // 2
         nc.gpsimd.memset(v_sb[0][:, :, D:V_USED], 1.0)
@@ -57,8 +61,9 @@ def tile_longcontextattention_b_kernel(tc, base, q, k, v, offs, out):
         nc.sync.dma_start(q_sb[0][:, PAIR * P : N], q[0:D, PAIR * P : N])
         nc.sync.dma_start(offsets[:], offs)
         nc.sync.dma_start(window[0][:], base[0:D, :])
-        for h in range(1, H):
+        def load(h):
             rows = slice(h * D, (h + 1) * D)
+            allocate()
             nc.gpsimd.memset(v_sb[h][:, :, D:V_USED], 1.0)
             nc.sync.dma_start(q_sb[h][:], q[rows, :])
             nc.sync.dma_start(k_sb[h][:], k[rows, :])
@@ -114,6 +119,8 @@ def tile_longcontextattention_b_kernel(tc, base, q, k, v, offs, out):
                 score(score_tiles[-1], x, h, pair, b0)
         complete = None
         for n, (h, pair, b0, blocks) in enumerate(steps):
+            if (pair, b0) == (0, 0) and h + 1 < H:
+                load(h + 1)
             e = exps.tile([P, STEP_BLOCKS, PAIR * P], BF16, name="e")
             nc.scalar.activation(e[:, 0:blocks, :], score_tiles[n][:, 0:blocks, :], EXP, scale=1.0 / math.sqrt(D))
 

@@ -11,7 +11,8 @@ STEP_BLOCKS = 2
 PAIRS = N // (PAIR * P)
 AHEAD = 3
 FLIPS = 2 * PAIR
-FLIP_LATE = 1
+FLIP_LATE = 3
+LAST_FLIP_LATE = 2
 V_PITCH = 256
 V_USED = 144
 
@@ -127,15 +128,14 @@ def tile_longcontextattention_b_kernel(tc, base, q, k, v, offs, out):
             ahead = steps[n + AHEAD] if n + AHEAD < len(steps) else None
             if ahead:
                 score_tiles.append(scores.tile([P, STEP_BLOCKS, PAIR * P], F32, name="s_ps"))
-            number = STEP_BLOCKS * (b0 // STEP_BLOCKS - FLIP_LATE)
-            flipping = complete and 0 <= number < FLIPS
             if b0 == 0:
                 product = products.tile([P, PAIR, D + 1], F32, name="product")
             for x in range(STEP_BLOCKS):
                 if ahead and x < ahead[3]:
                     score(score_tiles[-1], x, *ahead[:3])
-                if flipping:
-                    flip(number + x, *complete)
+                number = b0 + x - (LAST_FLIP_LATE if (h, pair) == (H - 1, PAIRS - 1) else FLIP_LATE)
+                if complete and 0 <= number < FLIPS:
+                    flip(number, *complete)
                 if x >= blocks:
                     continue
                 b = b0 + x

import math

import concourse.mybir as mybir
from concourse.masks import make_identity

H, D, S, T, N = 4, 128, 2048, 2048, 1024
P = 128
KEY_BLOCKS = T // P
PAIR = 2
STEP_BLOCKS = 2
PAIRS = N // (PAIR * P)
AHEAD = 3
FLIPS = 2 * PAIR
FLIP_LATE = 3
LAST_FLIP_LATE = 2
V_PITCH = 256
V_USED = 144

FLOPS = 4 * H * D * T * N

BF16, F32, U16 = mybir.dt.bfloat16, mybir.dt.float32, mybir.dt.uint16
EXP = mybir.ActivationFunctionType.Exp
MULT = mybir.AluOpType.mult


def tile_longcontextattention_b_kernel(tc, base, q, k, v, offs, out):
    nc = tc.nc
    v_blocks = v.rearrange("(b p) c -> p b c", p=P)
    with (
        tc.tile_pool(name="held", bufs=1) as held,
        tc.tile_pool(name="inputs", bufs=2) as inputs,
        tc.tile_pool(name="exps", bufs=2 * (AHEAD + 1)) as exps,
        tc.tile_pool(name="queries_first", bufs=2) as queries_first,
        tc.tile_pool(name="channels_first", bufs=2) as channels_first,
        tc.psum_pool(name="scores", bufs=AHEAD + 1) as scores,
        tc.psum_pool(name="products", bufs=2) as products,
        tc.psum_pool(name="flips", bufs=1) as flips,
    ):
        offsets = held.tile([P, N // 16], U16, name="offsets")

        q_sb, k_sb, v_sb, window = [], [], [], []

        def allocate():
            q_sb.append(inputs.tile([P, N], BF16, name="q"))
            k_sb.append(inputs.tile([P, T], BF16, name="k"))
            v_sb.append(inputs.tile([P, KEY_BLOCKS, V_PITCH], BF16, name="v"))
            window.append(inputs.tile([P, S], F32, name="window"))

        allocate()

        quarter, half = T // 4, T // 2
        nc.gpsimd.memset(v_sb[0][:, :, D:V_USED], 1.0)
        nc.sync.dma_start(k_sb[0][:, 0:quarter], k[0:D, 0:quarter])
        nc.scalar.dma_start(q_sb[0][:, 0 : PAIR * P], q[0:D, 0 : PAIR * P])
        nc.sync.dma_start(k_sb[0][:, quarter:half], k[0:D, quarter:half])
        nc.scalar.dma_start(v_sb[0][:, 0 : KEY_BLOCKS // 4, 0:D], v_blocks[:, 0 : KEY_BLOCKS // 4, 0:D])
        nc.sync.dma_start(
            v_sb[0][:, KEY_BLOCKS // 4 : KEY_BLOCKS // 2, 0:D], v_blocks[:, KEY_BLOCKS // 4 : KEY_BLOCKS // 2, 0:D]
        )
        nc.sync.dma_start(k_sb[0][:, half:T], k[0:D, half:T])
        nc.sync.dma_start(v_sb[0][:, KEY_BLOCKS // 2 : KEY_BLOCKS, 0:D], v_blocks[:, KEY_BLOCKS // 2 : KEY_BLOCKS, 0:D])
        nc.sync.dma_start(q_sb[0][:, PAIR * P : N], q[0:D, PAIR * P : N])
        nc.sync.dma_start(offsets[:], offs)
        nc.sync.dma_start(window[0][:], base[0:D, :])
        def load(h):
            rows = slice(h * D, (h + 1) * D)
            allocate()
            nc.gpsimd.memset(v_sb[h][:, :, D:V_USED], 1.0)
            nc.sync.dma_start(q_sb[h][:], q[rows, :])
            nc.sync.dma_start(k_sb[h][:], k[rows, :])
            nc.sync.dma_start(v_sb[h][:, :, 0:D], v_blocks[:, :, rows])
            nc.sync.dma_start(window[h][:], base[rows, :])

        identity = held.tile([P, P], F32, name="identity")
        make_identity(nc, identity[:])

        def score(s_ps, x, h, pair, b0):
            b = b0 + x
            nc.tensor.matmul(
                s_ps[:, x, :],
                k_sb[h][:, b * P : (b + 1) * P],
                q_sb[h][:, pair * PAIR * P : (pair + 1) * PAIR * P],
                start=True,
                stop=True,
            )

        def place(h, pair, num_ps, r_ps):
            r_sb = channels_first.tile([P, PAIR * P], F32, name="r_sb")
            nc.vector.tensor_copy(r_sb[:], r_ps[:])
            num_sb = channels_first.tile([P, PAIR * P], F32, name="num_sb")
            nc.vector.tensor_copy(num_sb[:], num_ps[:])
            columns = PAIR * P // 16
            nc.vector.tensor_tensor(
                window[h][:].indirect(offsets[:, pair * columns : (pair + 1) * columns]), num_sb[:], r_sb[:], MULT
            )
            if pair == PAIRS - 1:
                nc.sync.dma_start(out[h * D : (h + 1) * D, :], window[h][:])

        def flip(number, h, pair, num_t, r_t, num_ps, r_ps):
            i = number % PAIR
            columns = slice(i * P, (i + 1) * P)
            if number < PAIR:
                nc.tensor.transpose(r_ps[:, columns], r_t[:, i, :].to_broadcast([P, P]), identity[:])
            else:
                nc.tensor.transpose(num_ps[:, columns], num_t[:, i, :], identity[:])
            if number == FLIPS - 1:
                place(h, pair, num_ps, r_ps)

        def halves(h, pair, b0, blocks):
            return [(h, pair, b0, 1), (h, pair, b0 + 1, 1)]

        steps = [
            (h, pair, b0, STEP_BLOCKS) for h in range(H) for pair in range(PAIRS) for b0 in range(0, KEY_BLOCKS, STEP_BLOCKS)
        ]
        steps = halves(*steps[0]) + steps[1:-1] + halves(*steps[-1])
        score_tiles = []
        for h, pair, b0, blocks in steps[:AHEAD]:
            score_tiles.append(scores.tile([P, STEP_BLOCKS, PAIR * P], F32, name="s_ps"))
            for x in range(blocks):
                score(score_tiles[-1], x, h, pair, b0)
        complete = None
        for n, (h, pair, b0, blocks) in enumerate(steps):
            if (pair, b0) == (0, 0) and h + 1 < H:
                load(h + 1)
            e = exps.tile([P, STEP_BLOCKS, PAIR * P], BF16, name="e")
            nc.scalar.activation(e[:, 0:blocks, :], score_tiles[n][:, 0:blocks, :], EXP, scale=1.0 / math.sqrt(D))

            ahead = steps[n + AHEAD] if n + AHEAD < len(steps) else None
            if ahead:
                score_tiles.append(scores.tile([P, STEP_BLOCKS, PAIR * P], F32, name="s_ps"))
            if b0 == 0:
                product = products.tile([P, PAIR, D + 1], F32, name="product")
            for x in range(STEP_BLOCKS):
                if ahead and x < ahead[3]:
                    score(score_tiles[-1], x, *ahead[:3])
                number = b0 + x - (LAST_FLIP_LATE if (h, pair) == (H - 1, PAIRS - 1) else FLIP_LATE)
                if complete and 0 <= number < FLIPS:
                    flip(number, *complete)
                if x >= blocks:
                    continue
                b = b0 + x
                for i in range(PAIR):
                    nc.tensor.matmul(
                        product[:, i, :],
                        e[:, x, i * P : (i + 1) * P],
                        v_sb[h][:, b, 0 : D + 1],
                        start=(b == 0 and i == 0),
                        stop=(b == KEY_BLOCKS - 1 and i == PAIR - 1),
                    )

            if b0 + blocks == KEY_BLOCKS:
                r_t = queries_first.tile([P, PAIR, 1], F32, name="r_t")
                nc.vector.reciprocal(r_t[:], product[:, :, D : D + 1])
                num_t = queries_first.tile([P, PAIR, D], F32, name="num_t")
                nc.vector.tensor_copy(num_t[:], product[:, :, 0:D])
                r_ps = flips.tile([P, PAIR * P], F32, name="r_ps")
                num_ps = flips.tile([P, PAIR * P], F32, name="num_ps")
                complete = (h, pair, num_t, r_t, num_ps, r_ps)
        for number in range(FLIPS):
            flip(number, *complete)
